import numpy as np
import ml_dtypes

BF16 = ml_dtypes.bfloat16


def bf(x):
    return np.asarray(x, np.float32).astype(BF16)


def f32(x):
    return np.asarray(x, np.float32)


def f64(x):
    return np.asarray(x).astype(np.float64)


def striped(idx):
    return np.tile(idx.reshape(-1, 16).T, (8, 1))


V, D, M, N = 1024, 128, 512, 2048


def setup_inputs():
    return {"table": bf(np.random.standard_normal((V, D))), "w": bf(np.random.standard_normal((D, M)) / np.sqrt(D)), "offs": striped(np.random.permutation(np.tile(np.arange(V), 2))[:N])}


def reference(table, w, offs):
    idx = offs[:16].T.reshape(-1)
    return f64(w).T @ f64(table)[idx].T

@@ -1,0 +1,48 @@
+import concourse.mybir as mybir
+from concourse.masks import make_identity
+
+P = 128
+V = 1024
+M = 512
+N = 2048
+PIECE = 512
+FLOPS = 2 * P * M * N
+
+BF16, F32, U16 = mybir.dt.bfloat16, mybir.dt.float32, mybir.dt.uint16
+COPY = mybir.ActivationFunctionType.Copy
+
+
+def tile_bdh_kernel(tc, table, w, offs, out):
+    nc = tc.nc
+    with (
+        tc.tile_pool(name="held", bufs=1) as held,
+        tc.tile_pool(name="stage", bufs=8) as stage,
+        tc.psum_pool(name="flip", bufs=1) as flip,
+        tc.psum_pool(name="acc", bufs=6) as acc,
+    ):
+        words = held.tile([P, V // P, P], BF16, name="words")
+        nc.scalar.dma_start(words[:], table.rearrange("(a p) d -> p a d", p=P))
+        offsets = held.tile([P, N // 16], U16, name="offsets")
+        nc.sync.dma_start(offsets[:], offs)
+        weights = held.tile([P, M], BF16, name="weights")
+        nc.sync.dma_start(weights[:], w)
+
+        identity = held.tile([P, P], BF16, name="identity")
+        make_identity(nc, identity[:])
+        flipped = flip.tile([P, V], BF16, name="flipped")
+        for a in range(V // P):
+            nc.tensor.transpose(flipped[:, a * P : (a + 1) * P], words[:, a, :], identity[:])
+        window = held.tile([P, V], BF16, name="window")
+        nc.vector.tensor_copy(window[:], flipped[:])
+
+        for j in range(N // PIECE):
+            looked_up = window[:].indirect(offsets[:, j * (PIECE // 16) : (j + 1) * (PIECE // 16)])
+            for m in range(M // P):
+                sums = acc.tile([P, PIECE], F32, name="sums")
+                nc.tensor.matmul(sums[:], weights[:, m * P : (m + 1) * P], looked_up, start=True, stop=True)
+                logits = stage.tile([P, PIECE], F32, name="logits")
+                if m % 2 == 0:
+                    nc.vector.tensor_copy(logits[:], sums[:])
+                else:
+                    nc.scalar.activation(logits[:], sums[:], COPY)
+                nc.sync.dma_start(out[m * P : (m + 1) * P, j * PIECE : (j + 1) * PIECE], logits[:])

@@ -7,6 +7,8 @@ M = 512
 N = 2048
 PIECE = 512
 FLOPS = 2 * P * M * N
+WARM_BEFORE = 6
+WARM_DURING_COPY = 2
 
 BF16, F32, U16 = mybir.dt.bfloat16, mybir.dt.float32, mybir.dt.uint16
 COPY = mybir.ActivationFunctionType.Copy
@@ -27,6 +29,12 @@ def tile_bdh_kernel(tc, table, w, offs, out):
         weights = held.tile([P, M], BF16, name="weights")
         nc.sync.dma_start(weights[:], w)
 
+        zeros = held.tile([P, PIECE], BF16, name="zeros")
+        nc.vector.memset(zeros[:], 0.0)
+        unread = flip.tile([P, PIECE], F32, name="unread")
+        for i in range(WARM_BEFORE):
+            nc.tensor.matmul(unread[:], zeros[:, 0:P], zeros[:], start=True, stop=True)
+
         identity = held.tile([P, P], BF16, name="identity")
         make_identity(nc, identity[:])
         flipped = flip.tile([P, V], BF16, name="flipped")
@@ -34,6 +42,8 @@ def tile_bdh_kernel(tc, table, w, offs, out):
             nc.tensor.transpose(flipped[:, a * P : (a + 1) * P], words[:, a, :], identity[:])
         window = held.tile([P, V], BF16, name="window")
         nc.vector.tensor_copy(window[:], flipped[:])
+        for i in range(WARM_DURING_COPY):
+            nc.tensor.matmul(unread[:], zeros[:, 0:P], zeros[:], start=True, stop=True)
 
         for j in range(N // PIECE):
             looked_up = window[:].indirect(offsets[:, j * (PIECE // 16) : (j + 1) * (PIECE // 16)])

@@ -7,8 +7,6 @@ M = 512
 N = 2048
 PIECE = 512
 FLOPS = 2 * P * M * N
-WARM_BEFORE = 6
-WARM_DURING_COPY = 2
 
 BF16, F32, U16 = mybir.dt.bfloat16, mybir.dt.float32, mybir.dt.uint16
 COPY = mybir.ActivationFunctionType.Copy
@@ -18,7 +16,7 @@ def tile_bdh_kernel(tc, table, w, offs, out):
     nc = tc.nc
     with (
         tc.tile_pool(name="held", bufs=1) as held,
-        tc.tile_pool(name="stage", bufs=8) as stage,
+        tc.tile_pool(name="stage", bufs=4) as stage,
         tc.psum_pool(name="flip", bufs=1) as flip,
         tc.psum_pool(name="acc", bufs=6) as acc,
     ):
@@ -29,12 +27,6 @@ def tile_bdh_kernel(tc, table, w, offs, out):
         weights = held.tile([P, M], BF16, name="weights")
         nc.sync.dma_start(weights[:], w)
 
-        zeros = held.tile([P, PIECE], BF16, name="zeros")
-        nc.vector.memset(zeros[:], 0.0)
-        unread = flip.tile([P, PIECE], F32, name="unread")
-        for i in range(WARM_BEFORE):
-            nc.tensor.matmul(unread[:], zeros[:, 0:P], zeros[:], start=True, stop=True)
-
         identity = held.tile([P, P], BF16, name="identity")
         make_identity(nc, identity[:])
         flipped = flip.tile([P, V], BF16, name="flipped")
@@ -42,17 +34,17 @@ def tile_bdh_kernel(tc, table, w, offs, out):
             nc.tensor.transpose(flipped[:, a * P : (a + 1) * P], words[:, a, :], identity[:])
         window = held.tile([P, V], BF16, name="window")
         nc.vector.tensor_copy(window[:], flipped[:])
-        for i in range(WARM_DURING_COPY):
-            nc.tensor.matmul(unread[:], zeros[:, 0:P], zeros[:], start=True, stop=True)
 
-        for j in range(N // PIECE):
-            looked_up = window[:].indirect(offsets[:, j * (PIECE // 16) : (j + 1) * (PIECE // 16)])
-            for m in range(M // P):
+        for m in range(M // P):
+            logits = stage.tile([P, N], F32, name="logits")
+            for j in range(N // PIECE):
+                here = slice(j * PIECE, (j + 1) * PIECE)
+                looked_up = window[:].indirect(offsets[:, j * (PIECE // 16) : (j + 1) * (PIECE // 16)])
                 sums = acc.tile([P, PIECE], F32, name="sums")
                 nc.tensor.matmul(sums[:], weights[:, m * P : (m + 1) * P], looked_up, start=True, stop=True)
-                logits = stage.tile([P, PIECE], F32, name="logits")
-                if m % 2 == 0:
-                    nc.vector.tensor_copy(logits[:], sums[:])
+                if j % 2 == 0:
+                    nc.vector.tensor_copy(logits[:, here], sums[:])
                 else:
-                    nc.scalar.activation(logits[:], sums[:], COPY)
-                nc.sync.dma_start(out[m * P : (m + 1) * P, j * PIECE : (j + 1) * PIECE], logits[:])
+                    nc.scalar.activation(logits[:, here], sums[:], COPY)
+                    pair = slice((j - 1) * PIECE, (j + 1) * PIECE)
+                    nc.sync.dma_start(out[m * P : (m + 1) * P, pair], logits[:, pair])

@@ -6,6 +6,8 @@ V = 1024
 M = 512
 N = 2048
 PIECE = 512
+CHUNKS = 4
+CHUNK = V // CHUNKS
 FLOPS = 2 * P * M * N
 
 BF16, F32, U16 = mybir.dt.bfloat16, mybir.dt.float32, mybir.dt.uint16
@@ -17,23 +19,31 @@ def tile_bdh_kernel(tc, table, w, offs, out):
     with (
         tc.tile_pool(name="held", bufs=1) as held,
         tc.tile_pool(name="stage", bufs=4) as stage,
-        tc.psum_pool(name="flip", bufs=1) as flip,
-        tc.psum_pool(name="acc", bufs=6) as acc,
+        tc.psum_pool(name="flip", bufs=4) as flip,
+        tc.psum_pool(name="acc", bufs=4) as acc,
     ):
-        words = held.tile([P, V // P, P], BF16, name="words")
-        nc.scalar.dma_start(words[:], table.rearrange("(a p) d -> p a d", p=P))
+        table_chunks = table.rearrange("(c a p) d -> c p a d", a=CHUNK // P, p=P)
+        words = []
+        for c in range(CHUNKS):
+            words.append(held.tile([P, CHUNK // P, P], BF16, name=f"words{c}"))
+            queue = nc.sync if c % 2 == 0 else nc.scalar
+            queue.dma_start(words[c][:], table_chunks[c])
         offsets = held.tile([P, N // 16], U16, name="offsets")
         nc.sync.dma_start(offsets[:], offs)
         weights = held.tile([P, M], BF16, name="weights")
-        nc.sync.dma_start(weights[:], w)
+        nc.scalar.dma_start(weights[:], w)
 
         identity = held.tile([P, P], BF16, name="identity")
         make_identity(nc, identity[:])
-        flipped = flip.tile([P, V], BF16, name="flipped")
-        for a in range(V // P):
-            nc.tensor.transpose(flipped[:, a * P : (a + 1) * P], words[:, a, :], identity[:])
         window = held.tile([P, V], BF16, name="window")
-        nc.vector.tensor_copy(window[:], flipped[:])
+        for c in range(CHUNKS):
+            flipped = flip.tile([P, CHUNK], BF16, name="flipped")
+            for a in range(CHUNK // P):
+                nc.tensor.transpose(flipped[:, a * P : (a + 1) * P], words[c][:, a, :], identity[:])
+            if c % 2 == 0:
+                nc.vector.tensor_copy(window[:, c * CHUNK : (c + 1) * CHUNK], flipped[:])
+            else:
+                nc.scalar.activation(window[:, c * CHUNK : (c + 1) * CHUNK], flipped[:], COPY)
 
         for m in range(M // P):
             logits = stage.tile([P, N], F32, name="logits")

@@ -56,5 +56,8 @@ def tile_bdh_kernel(tc, table, w, offs, out):
                     nc.vector.tensor_copy(logits[:, here], sums[:])
                 else:
                     nc.scalar.activation(logits[:, here], sums[:], COPY)
+                if m == 0 and j < 2:
+                    nc.sync.dma_start(out[m * P : (m + 1) * P, here], logits[:, here])
+                elif j % 2 == 1:
                     pair = slice((j - 1) * PIECE, (j + 1) * PIECE)
                     nc.sync.dma_start(out[m * P : (m + 1) * P, pair], logits[:, pair])

@@ -56,7 +56,7 @@ def tile_bdh_kernel(tc, table, w, offs, out):
                     nc.vector.tensor_copy(logits[:, here], sums[:])
                 else:
                     nc.scalar.activation(logits[:, here], sums[:], COPY)
-                if m == 0 and j < 2:
+                if m == M // P - 1 and j >= N // PIECE - 2:
                     nc.sync.dma_start(out[m * P : (m + 1) * P, here], logits[:, here])
                 elif j % 2 == 1:
                     pair = slice((j - 1) * PIECE, (j + 1) * PIECE)

@@ -56,8 +56,6 @@ def tile_bdh_kernel(tc, table, w, offs, out):
                     nc.vector.tensor_copy(logits[:, here], sums[:])
                 else:
                     nc.scalar.activation(logits[:, here], sums[:], COPY)
-                if m == M // P - 1 and j >= N // PIECE - 2:
-                    nc.sync.dma_start(out[m * P : (m + 1) * P, here], logits[:, here])
-                elif j % 2 == 1:
                     pair = slice((j - 1) * PIECE, (j + 1) * PIECE)
-                    nc.sync.dma_start(out[m * P : (m + 1) * P, pair], logits[:, pair])
+                    queue = nc.sync if j == 1 else nc.scalar
+                    queue.dma_start(out[m * P : (m + 1) * P, pair], logits[:, pair])

@@ -22,7 +22,7 @@ def tile_bdh_kernel(tc, table, w, offs, out):
         tc.psum_pool(name="flip", bufs=4) as flip,
         tc.psum_pool(name="acc", bufs=4) as acc,
     ):
-        table_chunks = table.rearrange("(c a p) d -> c p a d", a=CHUNK // P, p=P)
+        table_chunks = table.rearrange("(c p a) d -> c p a d", a=CHUNK // P, p=P)
         words = []
         for c in range(CHUNKS):
             words.append(held.tile([P, CHUNK // P, P], BF16, name=f"words{c}"))
@@ -40,10 +40,12 @@ def tile_bdh_kernel(tc, table, w, offs, out):
             flipped = flip.tile([P, CHUNK], BF16, name="flipped")
             for a in range(CHUNK // P):
                 nc.tensor.transpose(flipped[:, a * P : (a + 1) * P], words[c][:, a, :], identity[:])
+            in_order = flipped[:].rearrange("d (a p) -> d p a", a=CHUNK // P)
+            columns = window[:, c * CHUNK : (c + 1) * CHUNK].rearrange("d (p a) -> d p a", a=CHUNK // P)
             if c % 2 == 0:
-                nc.vector.tensor_copy(window[:, c * CHUNK : (c + 1) * CHUNK], flipped[:])
+                nc.vector.tensor_copy(columns, in_order)
             else:
-                nc.scalar.activation(window[:, c * CHUNK : (c + 1) * CHUNK], flipped[:], COPY)
+                nc.scalar.activation(columns, in_order, COPY)
 
         for m in range(M // P):
             logits = stage.tile([P, N], F32, name="logits")
@@ -57,5 +59,4 @@ def tile_bdh_kernel(tc, table, w, offs, out):
                 else:
                     nc.scalar.activation(logits[:, here], sums[:], COPY)
                     pair = slice((j - 1) * PIECE, (j + 1) * PIECE)
-                    queue = nc.sync if j == 1 else nc.scalar
-                    queue.dma_start(out[m * P : (m + 1) * P, pair], logits[:, pair])
+                    nc.sync.dma_start(out[m * P : (m + 1) * P, pair], logits[:, pair])

@@ -42,10 +42,7 @@ def tile_bdh_kernel(tc, table, w, offs, out):
                 nc.tensor.transpose(flipped[:, a * P : (a + 1) * P], words[c][:, a, :], identity[:])
             in_order = flipped[:].rearrange("d (a p) -> d p a", a=CHUNK // P)
             columns = window[:, c * CHUNK : (c + 1) * CHUNK].rearrange("d (p a) -> d p a", a=CHUNK // P)
-            if c % 2 == 0:
-                nc.vector.tensor_copy(columns, in_order)
-            else:
-                nc.scalar.activation(columns, in_order, COPY)
+            nc.vector.tensor_copy(columns, in_order)
 
         for m in range(M // P):
             logits = stage.tile([P, N], F32, name="logits")

@@ -33,6 +33,11 @@ def tile_bdh_kernel(tc, table, w, offs, out):
         weights = held.tile([P, M], BF16, name="weights")
         nc.scalar.dma_start(weights[:], w)
 
+        zero = held.tile([P, 1], F32, name="zero")
+        nc.vector.memset(zero[:], 0.0)
+        warmed = held.tile([P, 1], F32, name="warmed")
+        nc.scalar.activation(warmed[:], zero[:], COPY)
+
         identity = held.tile([P, P], BF16, name="identity")
         make_identity(nc, identity[:])
         window = held.tile([P, V], BF16, name="window")

@@ -11,7 +11,6 @@ CHUNK = V // CHUNKS
 FLOPS = 2 * P * M * N
 
 BF16, F32, U16 = mybir.dt.bfloat16, mybir.dt.float32, mybir.dt.uint16
-COPY = mybir.ActivationFunctionType.Copy
 
 
 def tile_bdh_kernel(tc, table, w, offs, out):
@@ -33,11 +32,6 @@ def tile_bdh_kernel(tc, table, w, offs, out):
         weights = held.tile([P, M], BF16, name="weights")
         nc.scalar.dma_start(weights[:], w)
 
-        zero = held.tile([P, 1], F32, name="zero")
-        nc.vector.memset(zero[:], 0.0)
-        warmed = held.tile([P, 1], F32, name="warmed")
-        nc.scalar.activation(warmed[:], zero[:], COPY)
-
         identity = held.tile([P, P], BF16, name="identity")
         make_identity(nc, identity[:])
         window = held.tile([P, V], BF16, name="window")
@@ -56,9 +50,8 @@ def tile_bdh_kernel(tc, table, w, offs, out):
                 looked_up = window[:].indirect(offsets[:, j * (PIECE // 16) : (j + 1) * (PIECE // 16)])
                 sums = acc.tile([P, PIECE], F32, name="sums")
                 nc.tensor.matmul(sums[:], weights[:, m * P : (m + 1) * P], looked_up, start=True, stop=True)
-                if j % 2 == 0:
-                    nc.vector.tensor_copy(logits[:, here], sums[:])
-                else:
-                    nc.scalar.activation(logits[:, here], sums[:], COPY)
+                nc.vector.tensor_copy(logits[:, here], sums[:])
+                if j % 2 == 1:
                     pair = slice((j - 1) * PIECE, (j + 1) * PIECE)
-                    nc.sync.dma_start(out[m * P : (m + 1) * P, pair], logits[:, pair])
+                    queue = nc.scalar if j == 1 else nc.sync
+                    queue.dma_start(out[m * P : (m + 1) * P, pair], logits[:, pair])

@@ -6,8 +6,7 @@ V = 1024
 M = 512
 N = 2048
 PIECE = 512
-CHUNKS = 4
-CHUNK = V // CHUNKS
+PARTS = ((0, 2), (2 * P, 2), (4 * P, 1), (5 * P, 1), (6 * P, 1), (7 * P, 1))
 FLOPS = 2 * P * M * N
 
 BF16, F32, U16 = mybir.dt.bfloat16, mybir.dt.float32, mybir.dt.uint16
@@ -18,15 +17,15 @@ def tile_bdh_kernel(tc, table, w, offs, out):
     with (
         tc.tile_pool(name="held", bufs=1) as held,
         tc.tile_pool(name="stage", bufs=4) as stage,
-        tc.psum_pool(name="flip", bufs=4) as flip,
-        tc.psum_pool(name="acc", bufs=4) as acc,
+        tc.psum_pool(name="banks", bufs=8) as banks,
     ):
-        table_chunks = table.rearrange("(c p a) d -> c p a d", a=CHUNK // P, p=P)
         words = []
-        for c in range(CHUNKS):
-            words.append(held.tile([P, CHUNK // P, P], BF16, name=f"words{c}"))
-            queue = nc.sync if c % 2 == 0 else nc.scalar
-            queue.dma_start(words[c][:], table_chunks[c])
+        for n, (first, a_count) in enumerate(PARTS):
+            part = held.tile([P, a_count, P], BF16, name=f"words{n}")
+            rows = table[first : first + a_count * P, :]
+            queue = nc.sync if n % 2 == 0 else nc.scalar
+            queue.dma_start(part[:], rows.rearrange("(p a) d -> p a d", a=a_count))
+            words.append(part)
         offsets = held.tile([P, N // 16], U16, name="offsets")
         nc.sync.dma_start(offsets[:], offs)
         weights = held.tile([P, M], BF16, name="weights")
@@ -35,12 +34,12 @@ def tile_bdh_kernel(tc, table, w, offs, out):
         identity = held.tile([P, P], BF16, name="identity")
         make_identity(nc, identity[:])
         window = held.tile([P, V], BF16, name="window")
-        for c in range(CHUNKS):
-            flipped = flip.tile([P, CHUNK], BF16, name="flipped")
-            for a in range(CHUNK // P):
-                nc.tensor.transpose(flipped[:, a * P : (a + 1) * P], words[c][:, a, :], identity[:])
-            in_order = flipped[:].rearrange("d (a p) -> d p a", a=CHUNK // P)
-            columns = window[:, c * CHUNK : (c + 1) * CHUNK].rearrange("d (p a) -> d p a", a=CHUNK // P)
+        for (first, a_count), part in zip(PARTS, words):
+            flipped = banks.tile([P, a_count * P], BF16, name="flipped", tag="bank")
+            for a in range(a_count):
+                nc.tensor.transpose(flipped[:, a * P : (a + 1) * P], part[:, a, :], identity[:])
+            in_order = flipped[:].rearrange("d (a p) -> d p a", a=a_count)
+            columns = window[:, first : first + a_count * P].rearrange("d (p a) -> d p a", a=a_count)
             nc.vector.tensor_copy(columns, in_order)
 
         for m in range(M // P):
@@ -48,7 +47,7 @@ def tile_bdh_kernel(tc, table, w, offs, out):
             for j in range(N // PIECE):
                 here = slice(j * PIECE, (j + 1) * PIECE)
                 looked_up = window[:].indirect(offsets[:, j * (PIECE // 16) : (j + 1) * (PIECE // 16)])
-                sums = acc.tile([P, PIECE], F32, name="sums")
+                sums = banks.tile([P, PIECE], F32, name="sums", tag="bank")
                 nc.tensor.matmul(sums[:], weights[:, m * P : (m + 1) * P], looked_up, start=True, stop=True)
                 nc.vector.tensor_copy(logits[:, here], sums[:])
                 if j % 2 == 1:

@@ -6,6 +6,7 @@ V = 1024
 M = 512
 N = 2048
 PIECE = 512
+PAIR = 2 * PIECE
 PARTS = ((0, 2), (2 * P, 2), (4 * P, 1), (5 * P, 1), (6 * P, 1), (7 * P, 1))
 FLOPS = 2 * P * M * N
 
@@ -42,15 +43,14 @@ def tile_bdh_kernel(tc, table, w, offs, out):
             columns = window[:, first : first + a_count * P].rearrange("d (p a) -> d p a", a=a_count)
             nc.vector.tensor_copy(columns, in_order)
 
-        for m in range(M // P):
-            logits = stage.tile([P, N], F32, name="logits")
-            for j in range(N // PIECE):
-                here = slice(j * PIECE, (j + 1) * PIECE)
-                looked_up = window[:].indirect(offsets[:, j * (PIECE // 16) : (j + 1) * (PIECE // 16)])
-                sums = banks.tile([P, PIECE], F32, name="sums", tag="bank")
-                nc.tensor.matmul(sums[:], weights[:, m * P : (m + 1) * P], looked_up, start=True, stop=True)
-                nc.vector.tensor_copy(logits[:, here], sums[:])
-                if j % 2 == 1:
-                    pair = slice((j - 1) * PIECE, (j + 1) * PIECE)
-                    queue = nc.scalar if j == 1 else nc.sync
-                    queue.dma_start(out[m * P : (m + 1) * P, pair], logits[:, pair])
+        for pair in range(N // PAIR):
+            for m in range(M // P):
+                logits = stage.tile([P, PAIR], F32, name="logits")
+                for half in range(PAIR // PIECE):
+                    first = pair * PAIR + half * PIECE
+                    looked_up = window[:].indirect(offsets[:, first // 16 : (first + PIECE) // 16])
+                    sums = banks.tile([P, PIECE], F32, name="sums", tag="bank")
+                    nc.tensor.matmul(sums[:], weights[:, m * P : (m + 1) * P], looked_up, start=True, stop=True)
+                    nc.vector.tensor_copy(logits[:, half * PIECE : (half + 1) * PIECE], sums[:])
+                queue = nc.scalar if m % 2 == 0 else nc.sync
+                queue.dma_start(out[m * P : (m + 1) * P, pair * PAIR : (pair + 1) * PAIR], logits[:])

import concourse.mybir as mybir
from concourse.masks import make_identity

P = 128
V = 1024
M = 512
N = 2048
PIECE = 512
PAIR = 2 * PIECE
PARTS = ((0, 2), (2 * P, 2), (4 * P, 1), (5 * P, 1), (6 * P, 1), (7 * P, 1))
FLOPS = 2 * P * M * N

BF16, F32, U16 = mybir.dt.bfloat16, mybir.dt.float32, mybir.dt.uint16


def tile_bdh_kernel(tc, table, w, offs, out):
    nc = tc.nc
    with (
        tc.tile_pool(name="held", bufs=1) as held,
        tc.tile_pool(name="stage", bufs=4) as stage,
        tc.psum_pool(name="banks", bufs=8) as banks,
    ):
        words = []
        for n, (first, a_count) in enumerate(PARTS):
            part = held.tile([P, a_count, P], BF16, name=f"words{n}")
            rows = table[first : first + a_count * P, :]
            queue = nc.sync if n % 2 == 0 else nc.scalar
            queue.dma_start(part[:], rows.rearrange("(p a) d -> p a d", a=a_count))
            words.append(part)
        offsets = held.tile([P, N // 16], U16, name="offsets")
        nc.sync.dma_start(offsets[:], offs)
        weights = held.tile([P, M], BF16, name="weights")
        nc.scalar.dma_start(weights[:], w)

        identity = held.tile([P, P], BF16, name="identity")
        make_identity(nc, identity[:])
        window = held.tile([P, V], BF16, name="window")
        for (first, a_count), part in zip(PARTS, words):
            flipped = banks.tile([P, a_count * P], BF16, name="flipped", tag="bank")
            for a in range(a_count):
                nc.tensor.transpose(flipped[:, a * P : (a + 1) * P], part[:, a, :], identity[:])
            in_order = flipped[:].rearrange("d (a p) -> d p a", a=a_count)
            columns = window[:, first : first + a_count * P].rearrange("d (p a) -> d p a", a=a_count)
            nc.vector.tensor_copy(columns, in_order)

        for pair in range(N // PAIR):
            for m in range(M // P):
                logits = stage.tile([P, PAIR], F32, name="logits")
                for half in range(PAIR // PIECE):
                    first = pair * PAIR + half * PIECE
                    looked_up = window[:].indirect(offsets[:, first // 16 : (first + PIECE) // 16])
                    sums = banks.tile([P, PIECE], F32, name="sums", tag="bank")
                    nc.tensor.matmul(sums[:], weights[:, m * P : (m + 1) * P], looked_up, start=True, stop=True)
                    nc.vector.tensor_copy(logits[:, half * PIECE : (half + 1) * PIECE], sums[:])
                queue = nc.scalar if m % 2 == 0 else nc.sync
                queue.dma_start(out[m * P : (m + 1) * P, pair * PAIR : (pair + 1) * PAIR], logits[:])
